import numpy as np
import ml_dtypes

BF16 = ml_dtypes.bfloat16


def bf(x):
    return np.asarray(x, np.float32).astype(BF16)


def f32(x):
    return np.asarray(x, np.float32)


def f64(x):
    return np.asarray(x).astype(np.float64)


def striped(idx):
    return np.tile(idx.reshape(-1, 16).T, (8, 1))


D, S, N = 128, 1024, 256
R_LO, R_HI = 0.4, 0.8


def in_ball(cols):
    v = np.random.standard_normal((D, cols))
    r = np.random.uniform(R_LO, R_HI, (1, cols))
    return f32(v / np.sqrt(np.sum(v * v, axis=0, keepdims=True)) * r)


def setup_inputs():
    return {"centers": in_ball(S), "z": in_ball(N), "offs": striped(np.random.permutation(np.tile(np.arange(S), 2))[:N])}


def reference(centers, z, offs):
    idx = offs[:16].T.reshape(-1)
    cs = f64(centers)[:, idx]
    y = f64(z)
    x2 = np.sum(cs * cs, axis=0, keepdims=True)
    y2 = np.sum(y * y, axis=0, keepdims=True)
    cz = np.sum(cs * y, axis=0, keepdims=True)
    num = (1.0 - x2) * y - (1.0 - 2.0 * cz + y2) * cs
    den = 1.0 - 2.0 * cz + x2 * y2
    return num / den

@@ -1,0 +1,83 @@
+import concourse.mybir as mybir
+
+P = 128
+S = 1024
+N = 256
+
+F32 = mybir.dt.float32
+U16 = mybir.dt.uint16
+MULT = mybir.AluOpType.mult
+ADD = mybir.AluOpType.add
+SUBTRACT = mybir.AluOpType.subtract
+ACT = mybir.ActivationFunctionType
+
+FLOPS = 11 * P * N
+BYTES = 3 * P * N * 4 + P * (N // 16) * 2
+
+
+def tile_factorizedjumpoperator_kernel(tc, centers, z, offs, out):
+    nc = tc.nc
+    with (
+        tc.tile_pool(name="held", bufs=1) as held,
+        tc.psum_pool(name="sums", bufs=1) as sums,
+    ):
+        offsets = held.tile([P, N // 16], U16, name="offsets")
+        nc.sync.dma_start(offsets[:], offs)
+        points = held.tile([P, N], F32, name="points")
+        nc.scalar.dma_start(points[:], z)
+        table = held.tile([P, S], F32, name="table")
+        nc.sync.dma_start(table[:], centers)
+
+        ones = held.tile([P, P], F32, name="ones")
+        nc.vector.memset(ones[:], 1.0)
+
+        points_squared = held.tile([P, N], F32, name="points_squared")
+        nc.vector.tensor_tensor(points_squared[:], points[:], points[:], MULT)
+        y2_sum = sums.tile([P, N], F32, name="y2_sum")
+        nc.tensor.matmul(y2_sum[:], ones[:], points_squared[:], start=True, stop=True)
+        y2 = held.tile([P, N], F32, name="y2")
+        nc.scalar.activation(y2[:], y2_sum[:], ACT.Copy)
+        y2_plus_1 = held.tile([P, N], F32, name="y2_plus_1")
+        nc.scalar.activation(y2_plus_1[:], y2_sum[:], ACT.Copy, bias=1.0)
+
+        centre_times_point = held.tile([P, N], F32, name="centre_times_point")
+        nc.vector.tensor_tensor(centre_times_point[:], table[:].indirect(offsets[:]), points[:], MULT)
+        cz_sum = sums.tile([P, N], F32, name="cz_sum")
+        nc.tensor.matmul(cz_sum[:], ones[:], centre_times_point[:], start=True, stop=True)
+
+        a = held.tile([P, N], F32, name="a")
+        nc.vector.scalar_tensor_tensor(a[:], cz_sum[:], -2.0, y2_plus_1[:], MULT, ADD)
+        a_centre = held.tile([P, N], F32, name="a_centre")
+        nc.vector.tensor_tensor(a_centre[:], table[:].indirect(offsets[:]), a[:], MULT)
+
+        a_centre_squared = held.tile([P, N], F32, name="a_centre_squared")
+        nc.scalar.activation(a_centre_squared[:], a_centre[:], ACT.Square)
+        a2_x2_sum = sums.tile([P, N], F32, name="a2_x2_sum")
+        nc.tensor.matmul(a2_x2_sum[:], ones[:], a_centre_squared[:], start=True, stop=True)
+
+        a2 = held.tile([P, N], F32, name="a2")
+        nc.vector.tensor_tensor(a2[:], a[:], a[:], MULT)
+        one_minus_2cz = held.tile([P, N], F32, name="one_minus_2cz")
+        nc.vector.tensor_tensor(one_minus_2cz[:], a[:], y2[:], SUBTRACT)
+        a2_one_minus_2cz = held.tile([P, N], F32, name="a2_one_minus_2cz")
+        nc.vector.tensor_tensor(a2_one_minus_2cz[:], a2[:], one_minus_2cz[:], MULT)
+        centre_term = held.tile([P, N], F32, name="centre_term")
+        nc.vector.tensor_tensor(centre_term[:], a2[:], a_centre[:], MULT)
+
+        a2_x2_y2 = held.tile([P, N], F32, name="a2_x2_y2")
+        nc.vector.tensor_tensor(a2_x2_y2[:], a2_x2_sum[:], y2[:], MULT)
+        denominator = held.tile([P, N], F32, name="denominator")
+        nc.vector.tensor_tensor(denominator[:], a2_x2_y2[:], a2_one_minus_2cz[:], ADD)
+        inverse = held.tile([P, N], F32, name="inverse")
+        nc.vector.reciprocal(inverse[:], denominator[:])
+
+        a2_gap = held.tile([P, N], F32, name="a2_gap")
+        nc.vector.tensor_tensor(a2_gap[:], a2[:], a2_x2_sum[:], SUBTRACT)
+        point_term = held.tile([P, N], F32, name="point_term")
+        nc.vector.tensor_tensor(point_term[:], a2_gap[:], points[:], MULT)
+        numerator = held.tile([P, N], F32, name="numerator")
+        nc.vector.tensor_tensor(numerator[:], point_term[:], centre_term[:], SUBTRACT)
+
+        result = held.tile([P, N], F32, name="result")
+        nc.vector.tensor_tensor(result[:], numerator[:], inverse[:], MULT)
+        nc.sync.dma_start(out, result[:])

@@ -30,53 +30,53 @@ def tile_factorizedjumpoperator_kernel(tc, centers, z, offs, out):
 
         ones = held.tile([P, P], F32, name="ones")
         nc.vector.memset(ones[:], 1.0)
+        minus_twos = held.tile([P, P], F32, name="minus_twos")
+        nc.vector.memset(minus_twos[:], -2.0)
 
         points_squared = held.tile([P, N], F32, name="points_squared")
         nc.vector.tensor_tensor(points_squared[:], points[:], points[:], MULT)
         y2_sum = sums.tile([P, N], F32, name="y2_sum")
         nc.tensor.matmul(y2_sum[:], ones[:], points_squared[:], start=True, stop=True)
-        y2 = held.tile([P, N], F32, name="y2")
-        nc.scalar.activation(y2[:], y2_sum[:], ACT.Copy)
         y2_plus_1 = held.tile([P, N], F32, name="y2_plus_1")
         nc.scalar.activation(y2_plus_1[:], y2_sum[:], ACT.Copy, bias=1.0)
+        y2 = held.tile([P, N], F32, name="y2")
+        nc.scalar.activation(y2[:], y2_sum[:], ACT.Copy)
+        twice_y2_plus_1 = held.tile([P, N], F32, name="twice_y2_plus_1")
+        nc.scalar.activation(twice_y2_plus_1[:], y2_sum[:], ACT.Copy, bias=2.0, scale=2.0)
 
         centre_times_point = held.tile([P, N], F32, name="centre_times_point")
         nc.vector.tensor_tensor(centre_times_point[:], table[:].indirect(offsets[:]), points[:], MULT)
-        cz_sum = sums.tile([P, N], F32, name="cz_sum")
-        nc.tensor.matmul(cz_sum[:], ones[:], centre_times_point[:], start=True, stop=True)
+        minus_2cz_sum = sums.tile([P, N], F32, name="minus_2cz_sum")
+        nc.tensor.matmul(minus_2cz_sum[:], minus_twos[:], centre_times_point[:], start=True, stop=True)
 
-        a = held.tile([P, N], F32, name="a")
-        nc.vector.scalar_tensor_tensor(a[:], cz_sum[:], -2.0, y2_plus_1[:], MULT, ADD)
-        a_centre = held.tile([P, N], F32, name="a_centre")
-        nc.vector.tensor_tensor(a_centre[:], table[:].indirect(offsets[:]), a[:], MULT)
+        centre_plus_point = held.tile([P, N], F32, name="centre_plus_point")
+        nc.vector.tensor_tensor(centre_plus_point[:], table[:].indirect(offsets[:]), points[:], ADD)
+        sum_squared = held.tile([P, N], F32, name="sum_squared")
+        nc.scalar.activation(sum_squared[:], centre_plus_point[:], ACT.Square)
+        t_sum = sums.tile([P, N], F32, name="t_sum")
+        nc.tensor.matmul(t_sum[:], ones[:], sum_squared[:], start=True, stop=True)
 
-        a_centre_squared = held.tile([P, N], F32, name="a_centre_squared")
-        nc.scalar.activation(a_centre_squared[:], a_centre[:], ACT.Square)
-        a2_x2_sum = sums.tile([P, N], F32, name="a2_x2_sum")
-        nc.tensor.matmul(a2_x2_sum[:], ones[:], a_centre_squared[:], start=True, stop=True)
-
-        a2 = held.tile([P, N], F32, name="a2")
-        nc.vector.tensor_tensor(a2[:], a[:], a[:], MULT)
-        one_minus_2cz = held.tile([P, N], F32, name="one_minus_2cz")
-        nc.vector.tensor_tensor(one_minus_2cz[:], a[:], y2[:], SUBTRACT)
-        a2_one_minus_2cz = held.tile([P, N], F32, name="a2_one_minus_2cz")
-        nc.vector.tensor_tensor(a2_one_minus_2cz[:], a2[:], one_minus_2cz[:], MULT)
+        coefficient = held.tile([P, N], F32, name="coefficient")
+        nc.vector.tensor_tensor(coefficient[:], minus_2cz_sum[:], y2_plus_1[:], ADD)
         centre_term = held.tile([P, N], F32, name="centre_term")
-        nc.vector.tensor_tensor(centre_term[:], a2[:], a_centre[:], MULT)
+        nc.vector.tensor_tensor(centre_term[:], table[:].indirect(offsets[:]), coefficient[:], MULT)
 
-        a2_x2_y2 = held.tile([P, N], F32, name="a2_x2_y2")
-        nc.vector.tensor_tensor(a2_x2_y2[:], a2_x2_sum[:], y2[:], MULT)
+        gap_plus_t = held.tile([P, N], F32, name="gap_plus_t")
+        nc.gpsimd.tensor_tensor(gap_plus_t[:], twice_y2_plus_1[:], coefficient[:], SUBTRACT)
+        gap = held.tile([P, N], F32, name="gap")
+        nc.vector.tensor_tensor(gap[:], gap_plus_t[:], t_sum[:], SUBTRACT)
+
+        gap_y2 = held.tile([P, N], F32, name="gap_y2")
+        nc.vector.tensor_tensor(gap_y2[:], gap[:], y2[:], MULT)
         denominator = held.tile([P, N], F32, name="denominator")
-        nc.vector.tensor_tensor(denominator[:], a2_x2_y2[:], a2_one_minus_2cz[:], ADD)
+        nc.vector.tensor_tensor(denominator[:], coefficient[:], gap_y2[:], SUBTRACT)
         inverse = held.tile([P, N], F32, name="inverse")
         nc.vector.reciprocal(inverse[:], denominator[:])
 
-        a2_gap = held.tile([P, N], F32, name="a2_gap")
-        nc.vector.tensor_tensor(a2_gap[:], a2[:], a2_x2_sum[:], SUBTRACT)
         point_term = held.tile([P, N], F32, name="point_term")
-        nc.vector.tensor_tensor(point_term[:], a2_gap[:], points[:], MULT)
+        nc.gpsimd.tensor_tensor(point_term[:], gap[:], points[:], MULT)
         numerator = held.tile([P, N], F32, name="numerator")
-        nc.vector.tensor_tensor(numerator[:], point_term[:], centre_term[:], SUBTRACT)
+        nc.gpsimd.tensor_tensor(numerator[:], point_term[:], centre_term[:], SUBTRACT)
 
         result = held.tile([P, N], F32, name="result")
         nc.vector.tensor_tensor(result[:], numerator[:], inverse[:], MULT)

@@ -14,6 +14,8 @@ ACT = mybir.ActivationFunctionType
 FLOPS = 11 * P * N
 BYTES = 3 * P * N * 4 + P * (N // 16) * 2
 
+BLOCK = 256
+
 
 def tile_factorizedjumpoperator_kernel(tc, centers, z, offs, out):
     nc = tc.nc
@@ -26,12 +28,17 @@ def tile_factorizedjumpoperator_kernel(tc, centers, z, offs, out):
         points = held.tile([P, N], F32, name="points")
         nc.scalar.dma_start(points[:], z)
         table = held.tile([P, S], F32, name="table")
-        nc.sync.dma_start(table[:], centers)
+        for b in range(S // BLOCK):
+            queue = nc.sync if b % 2 == 0 else nc.scalar
+            queue.dma_start(table[:, b * BLOCK : (b + 1) * BLOCK], centers[:, b * BLOCK : (b + 1) * BLOCK])
 
         ones = held.tile([P, P], F32, name="ones")
         nc.vector.memset(ones[:], 1.0)
         minus_twos = held.tile([P, P], F32, name="minus_twos")
         nc.vector.memset(minus_twos[:], -2.0)
+
+        table_set_first = held.tile([P, 1], F32, name="table_set_first")
+        nc.scalar.activation(table_set_first[:], ones[:, 0:1], ACT.Abs_reciprocal_sqrt)
 
         points_squared = held.tile([P, N], F32, name="points_squared")
         nc.vector.tensor_tensor(points_squared[:], points[:], points[:], MULT)
@@ -62,7 +69,7 @@ def tile_factorizedjumpoperator_kernel(tc, centers, z, offs, out):
         nc.vector.tensor_tensor(centre_term[:], table[:].indirect(offsets[:]), coefficient[:], MULT)
 
         gap_plus_t = held.tile([P, N], F32, name="gap_plus_t")
-        nc.gpsimd.tensor_tensor(gap_plus_t[:], twice_y2_plus_1[:], coefficient[:], SUBTRACT)
+        nc.vector.tensor_tensor(gap_plus_t[:], twice_y2_plus_1[:], coefficient[:], SUBTRACT)
         gap = held.tile([P, N], F32, name="gap")
         nc.vector.tensor_tensor(gap[:], gap_plus_t[:], t_sum[:], SUBTRACT)
 
@@ -70,13 +77,16 @@ def tile_factorizedjumpoperator_kernel(tc, centers, z, offs, out):
         nc.vector.tensor_tensor(gap_y2[:], gap[:], y2[:], MULT)
         denominator = held.tile([P, N], F32, name="denominator")
         nc.vector.tensor_tensor(denominator[:], coefficient[:], gap_y2[:], SUBTRACT)
+
+        inverse_root = held.tile([P, N], F32, name="inverse_root")
+        nc.scalar.activation(inverse_root[:], denominator[:], ACT.Abs_reciprocal_sqrt)
         inverse = held.tile([P, N], F32, name="inverse")
-        nc.vector.reciprocal(inverse[:], denominator[:])
+        nc.scalar.activation(inverse[:], inverse_root[:], ACT.Square)
 
         point_term = held.tile([P, N], F32, name="point_term")
-        nc.gpsimd.tensor_tensor(point_term[:], gap[:], points[:], MULT)
+        nc.vector.tensor_tensor(point_term[:], gap[:], points[:], MULT)
         numerator = held.tile([P, N], F32, name="numerator")
-        nc.gpsimd.tensor_tensor(numerator[:], point_term[:], centre_term[:], SUBTRACT)
+        nc.vector.tensor_tensor(numerator[:], point_term[:], centre_term[:], SUBTRACT)
 
         result = held.tile([P, N], F32, name="result")
         nc.vector.tensor_tensor(result[:], numerator[:], inverse[:], MULT)

@@ -40,51 +40,64 @@ def tile_factorizedjumpoperator_kernel(tc, centers, z, offs, out):
         table_set_first = held.tile([P, 1], F32, name="table_set_first")
         nc.scalar.activation(table_set_first[:], ones[:, 0:1], ACT.Abs_reciprocal_sqrt)
 
+        idle_work = sums.tile([P, P], F32, name="idle_work")
+
+        def keep_tensor_engine_busy(matmuls):
+            for _ in range(matmuls):
+                nc.tensor.matmul(idle_work[:], ones[:], ones[:], start=True, stop=True)
+
+        keep_tensor_engine_busy(6)
+
         points_squared = held.tile([P, N], F32, name="points_squared")
         nc.vector.tensor_tensor(points_squared[:], points[:], points[:], MULT)
         y2_sum = sums.tile([P, N], F32, name="y2_sum")
         nc.tensor.matmul(y2_sum[:], ones[:], points_squared[:], start=True, stop=True)
+        keep_tensor_engine_busy(3)
         y2_plus_1 = held.tile([P, N], F32, name="y2_plus_1")
         nc.scalar.activation(y2_plus_1[:], y2_sum[:], ACT.Copy, bias=1.0)
         y2 = held.tile([P, N], F32, name="y2")
         nc.scalar.activation(y2[:], y2_sum[:], ACT.Copy)
-        twice_y2_plus_1 = held.tile([P, N], F32, name="twice_y2_plus_1")
-        nc.scalar.activation(twice_y2_plus_1[:], y2_sum[:], ACT.Copy, bias=2.0, scale=2.0)
 
         centre_times_point = held.tile([P, N], F32, name="centre_times_point")
         nc.vector.tensor_tensor(centre_times_point[:], table[:].indirect(offsets[:]), points[:], MULT)
         minus_2cz_sum = sums.tile([P, N], F32, name="minus_2cz_sum")
         nc.tensor.matmul(minus_2cz_sum[:], minus_twos[:], centre_times_point[:], start=True, stop=True)
+        keep_tensor_engine_busy(3)
 
-        centre_plus_point = held.tile([P, N], F32, name="centre_plus_point")
-        nc.vector.tensor_tensor(centre_plus_point[:], table[:].indirect(offsets[:]), points[:], ADD)
-        sum_squared = held.tile([P, N], F32, name="sum_squared")
-        nc.scalar.activation(sum_squared[:], centre_plus_point[:], ACT.Square)
-        t_sum = sums.tile([P, N], F32, name="t_sum")
-        nc.tensor.matmul(t_sum[:], ones[:], sum_squared[:], start=True, stop=True)
+        a = held.tile([P, N], F32, name="a")
+        nc.vector.tensor_tensor(a[:], minus_2cz_sum[:], y2_plus_1[:], ADD)
+        a_centre = held.tile([P, N], F32, name="a_centre")
+        nc.vector.tensor_tensor(a_centre[:], table[:].indirect(offsets[:]), a[:], MULT)
 
-        coefficient = held.tile([P, N], F32, name="coefficient")
-        nc.vector.tensor_tensor(coefficient[:], minus_2cz_sum[:], y2_plus_1[:], ADD)
+        one_minus_2cz = held.tile([P, N], F32, name="one_minus_2cz")
+        nc.scalar.activation(one_minus_2cz[:], minus_2cz_sum[:], ACT.Copy, bias=1.0)
+        a2 = held.tile([P, N], F32, name="a2")
+        nc.scalar.activation(a2[:], a[:], ACT.Square)
+
+        a_centre_squared = held.tile([P, N], F32, name="a_centre_squared")
+        nc.scalar.activation(a_centre_squared[:], a_centre[:], ACT.Square)
+        a2_x2_sum = sums.tile([P, N], F32, name="a2_x2_sum")
+        nc.tensor.matmul(a2_x2_sum[:], ones[:], a_centre_squared[:], start=True, stop=True)
+
+        a2_one_minus_2cz = held.tile([P, N], F32, name="a2_one_minus_2cz")
+        nc.vector.tensor_tensor(a2_one_minus_2cz[:], a2[:], one_minus_2cz[:], MULT)
         centre_term = held.tile([P, N], F32, name="centre_term")
-        nc.vector.tensor_tensor(centre_term[:], table[:].indirect(offsets[:]), coefficient[:], MULT)
+        nc.vector.tensor_tensor(centre_term[:], a2[:], a_centre[:], MULT)
 
-        gap_plus_t = held.tile([P, N], F32, name="gap_plus_t")
-        nc.vector.tensor_tensor(gap_plus_t[:], twice_y2_plus_1[:], coefficient[:], SUBTRACT)
-        gap = held.tile([P, N], F32, name="gap")
-        nc.vector.tensor_tensor(gap[:], gap_plus_t[:], t_sum[:], SUBTRACT)
-
-        gap_y2 = held.tile([P, N], F32, name="gap_y2")
-        nc.vector.tensor_tensor(gap_y2[:], gap[:], y2[:], MULT)
+        a2_x2_y2 = held.tile([P, N], F32, name="a2_x2_y2")
+        nc.vector.tensor_tensor(a2_x2_y2[:], a2_x2_sum[:], y2[:], MULT)
         denominator = held.tile([P, N], F32, name="denominator")
-        nc.vector.tensor_tensor(denominator[:], coefficient[:], gap_y2[:], SUBTRACT)
+        nc.vector.tensor_tensor(denominator[:], a2_x2_y2[:], a2_one_minus_2cz[:], ADD)
 
         inverse_root = held.tile([P, N], F32, name="inverse_root")
         nc.scalar.activation(inverse_root[:], denominator[:], ACT.Abs_reciprocal_sqrt)
         inverse = held.tile([P, N], F32, name="inverse")
         nc.scalar.activation(inverse[:], inverse_root[:], ACT.Square)
 
+        a2_gap = held.tile([P, N], F32, name="a2_gap")
+        nc.vector.tensor_tensor(a2_gap[:], a2[:], a2_x2_sum[:], SUBTRACT)
         point_term = held.tile([P, N], F32, name="point_term")
-        nc.vector.tensor_tensor(point_term[:], gap[:], points[:], MULT)
+        nc.vector.tensor_tensor(point_term[:], a2_gap[:], points[:], MULT)
         numerator = held.tile([P, N], F32, name="numerator")
         nc.vector.tensor_tensor(numerator[:], point_term[:], centre_term[:], SUBTRACT)
 

@@ -37,22 +37,10 @@ def tile_factorizedjumpoperator_kernel(tc, centers, z, offs, out):
         minus_twos = held.tile([P, P], F32, name="minus_twos")
         nc.vector.memset(minus_twos[:], -2.0)
 
-        table_set_first = held.tile([P, 1], F32, name="table_set_first")
-        nc.scalar.activation(table_set_first[:], ones[:, 0:1], ACT.Abs_reciprocal_sqrt)
-
-        idle_work = sums.tile([P, P], F32, name="idle_work")
-
-        def keep_tensor_engine_busy(matmuls):
-            for _ in range(matmuls):
-                nc.tensor.matmul(idle_work[:], ones[:], ones[:], start=True, stop=True)
-
-        keep_tensor_engine_busy(6)
-
         points_squared = held.tile([P, N], F32, name="points_squared")
         nc.vector.tensor_tensor(points_squared[:], points[:], points[:], MULT)
         y2_sum = sums.tile([P, N], F32, name="y2_sum")
         nc.tensor.matmul(y2_sum[:], ones[:], points_squared[:], start=True, stop=True)
-        keep_tensor_engine_busy(3)
         y2_plus_1 = held.tile([P, N], F32, name="y2_plus_1")
         nc.scalar.activation(y2_plus_1[:], y2_sum[:], ACT.Copy, bias=1.0)
         y2 = held.tile([P, N], F32, name="y2")
@@ -62,44 +50,33 @@ def tile_factorizedjumpoperator_kernel(tc, centers, z, offs, out):
         nc.vector.tensor_tensor(centre_times_point[:], table[:].indirect(offsets[:]), points[:], MULT)
         minus_2cz_sum = sums.tile([P, N], F32, name="minus_2cz_sum")
         nc.tensor.matmul(minus_2cz_sum[:], minus_twos[:], centre_times_point[:], start=True, stop=True)
-        keep_tensor_engine_busy(3)
 
-        a = held.tile([P, N], F32, name="a")
-        nc.vector.tensor_tensor(a[:], minus_2cz_sum[:], y2_plus_1[:], ADD)
-        a_centre = held.tile([P, N], F32, name="a_centre")
-        nc.vector.tensor_tensor(a_centre[:], table[:].indirect(offsets[:]), a[:], MULT)
+        centre_plus_point = held.tile([P, N], F32, name="centre_plus_point")
+        nc.vector.tensor_tensor(centre_plus_point[:], table[:].indirect(offsets[:]), points[:], ADD)
+        sum_squared = held.tile([P, N], F32, name="sum_squared")
+        nc.vector.tensor_tensor(sum_squared[:], centre_plus_point[:], centre_plus_point[:], MULT)
+        t_sum = sums.tile([P, N], F32, name="t_sum")
+        nc.tensor.matmul(t_sum[:], ones[:], sum_squared[:], start=True, stop=True)
 
-        one_minus_2cz = held.tile([P, N], F32, name="one_minus_2cz")
-        nc.scalar.activation(one_minus_2cz[:], minus_2cz_sum[:], ACT.Copy, bias=1.0)
-        a2 = held.tile([P, N], F32, name="a2")
-        nc.scalar.activation(a2[:], a[:], ACT.Square)
+        coefficient = held.tile([P, N], F32, name="coefficient")
+        nc.vector.tensor_tensor(coefficient[:], y2_plus_1[:], minus_2cz_sum[:], ADD)
+        gap_plus_t = held.tile([P, N], F32, name="gap_plus_t")
+        nc.vector.tensor_tensor(gap_plus_t[:], y2_plus_1[:], minus_2cz_sum[:], SUBTRACT)
 
-        a_centre_squared = held.tile([P, N], F32, name="a_centre_squared")
-        nc.scalar.activation(a_centre_squared[:], a_centre[:], ACT.Square)
-        a2_x2_sum = sums.tile([P, N], F32, name="a2_x2_sum")
-        nc.tensor.matmul(a2_x2_sum[:], ones[:], a_centre_squared[:], start=True, stop=True)
-
-        a2_one_minus_2cz = held.tile([P, N], F32, name="a2_one_minus_2cz")
-        nc.vector.tensor_tensor(a2_one_minus_2cz[:], a2[:], one_minus_2cz[:], MULT)
+        gap = held.tile([P, N], F32, name="gap")
+        nc.vector.tensor_tensor(gap[:], gap_plus_t[:], t_sum[:], SUBTRACT)
         centre_term = held.tile([P, N], F32, name="centre_term")
-        nc.vector.tensor_tensor(centre_term[:], a2[:], a_centre[:], MULT)
-
-        a2_x2_y2 = held.tile([P, N], F32, name="a2_x2_y2")
-        nc.vector.tensor_tensor(a2_x2_y2[:], a2_x2_sum[:], y2[:], MULT)
-        denominator = held.tile([P, N], F32, name="denominator")
-        nc.vector.tensor_tensor(denominator[:], a2_x2_y2[:], a2_one_minus_2cz[:], ADD)
-
-        inverse_root = held.tile([P, N], F32, name="inverse_root")
-        nc.scalar.activation(inverse_root[:], denominator[:], ACT.Abs_reciprocal_sqrt)
-        inverse = held.tile([P, N], F32, name="inverse")
-        nc.scalar.activation(inverse[:], inverse_root[:], ACT.Square)
-
-        a2_gap = held.tile([P, N], F32, name="a2_gap")
-        nc.vector.tensor_tensor(a2_gap[:], a2[:], a2_x2_sum[:], SUBTRACT)
+        nc.vector.tensor_tensor(centre_term[:], table[:].indirect(offsets[:]), coefficient[:], MULT)
+        gap_y2 = held.tile([P, N], F32, name="gap_y2")
+        nc.vector.tensor_tensor(gap_y2[:], gap[:], y2[:], MULT)
         point_term = held.tile([P, N], F32, name="point_term")
-        nc.vector.tensor_tensor(point_term[:], a2_gap[:], points[:], MULT)
+        nc.vector.tensor_tensor(point_term[:], gap[:], points[:], MULT)
+        denominator = held.tile([P, N], F32, name="denominator")
+        nc.vector.tensor_tensor(denominator[:], coefficient[:], gap_y2[:], SUBTRACT)
         numerator = held.tile([P, N], F32, name="numerator")
         nc.vector.tensor_tensor(numerator[:], point_term[:], centre_term[:], SUBTRACT)
+        inverse = held.tile([P, N], F32, name="inverse")
+        nc.vector.reciprocal(inverse[:], denominator[:])
 
         result = held.tile([P, N], F32, name="result")
         nc.vector.tensor_tensor(result[:], numerator[:], inverse[:], MULT)

@@ -37,12 +37,16 @@ def tile_factorizedjumpoperator_kernel(tc, centers, z, offs, out):
         minus_twos = held.tile([P, P], F32, name="minus_twos")
         nc.vector.memset(minus_twos[:], -2.0)
 
+        minus_points = held.tile([P, N], F32, name="minus_points")
+        nc.vector.tensor_scalar_mul(minus_points[:], points[:], -1.0)
         points_squared = held.tile([P, N], F32, name="points_squared")
         nc.vector.tensor_tensor(points_squared[:], points[:], points[:], MULT)
         y2_sum = sums.tile([P, N], F32, name="y2_sum")
         nc.tensor.matmul(y2_sum[:], ones[:], points_squared[:], start=True, stop=True)
         y2_plus_1 = held.tile([P, N], F32, name="y2_plus_1")
         nc.scalar.activation(y2_plus_1[:], y2_sum[:], ACT.Copy, bias=1.0)
+        one_minus_y2 = held.tile([P, N], F32, name="one_minus_y2")
+        nc.scalar.activation(one_minus_y2[:], y2_sum[:], ACT.Copy, bias=1.0, scale=-1.0)
         y2 = held.tile([P, N], F32, name="y2")
         nc.scalar.activation(y2[:], y2_sum[:], ACT.Copy)
 
@@ -51,32 +55,33 @@ def tile_factorizedjumpoperator_kernel(tc, centers, z, offs, out):
         minus_2cz_sum = sums.tile([P, N], F32, name="minus_2cz_sum")
         nc.tensor.matmul(minus_2cz_sum[:], minus_twos[:], centre_times_point[:], start=True, stop=True)
 
-        centre_plus_point = held.tile([P, N], F32, name="centre_plus_point")
-        nc.vector.tensor_tensor(centre_plus_point[:], table[:].indirect(offsets[:]), points[:], ADD)
-        sum_squared = held.tile([P, N], F32, name="sum_squared")
-        nc.vector.tensor_tensor(sum_squared[:], centre_plus_point[:], centre_plus_point[:], MULT)
-        t_sum = sums.tile([P, N], F32, name="t_sum")
-        nc.tensor.matmul(t_sum[:], ones[:], sum_squared[:], start=True, stop=True)
+        centre_minus_point = held.tile([P, N], F32, name="centre_minus_point")
+        nc.vector.tensor_tensor(centre_minus_point[:], table[:].indirect(offsets[:]), minus_points[:], ADD)
+        difference_squared = held.tile([P, N], F32, name="difference_squared")
+        nc.vector.tensor_tensor(difference_squared[:], centre_minus_point[:], centre_minus_point[:], MULT)
+        distance_sum = sums.tile([P, N], F32, name="distance_sum")
+        nc.tensor.matmul(distance_sum[:], ones[:], difference_squared[:], start=True, stop=True)
 
         coefficient = held.tile([P, N], F32, name="coefficient")
         nc.vector.tensor_tensor(coefficient[:], y2_plus_1[:], minus_2cz_sum[:], ADD)
-        gap_plus_t = held.tile([P, N], F32, name="gap_plus_t")
-        nc.vector.tensor_tensor(gap_plus_t[:], y2_plus_1[:], minus_2cz_sum[:], SUBTRACT)
-
-        gap = held.tile([P, N], F32, name="gap")
-        nc.vector.tensor_tensor(gap[:], gap_plus_t[:], t_sum[:], SUBTRACT)
         centre_term = held.tile([P, N], F32, name="centre_term")
         nc.vector.tensor_tensor(centre_term[:], table[:].indirect(offsets[:]), coefficient[:], MULT)
-        gap_y2 = held.tile([P, N], F32, name="gap_y2")
-        nc.vector.tensor_tensor(gap_y2[:], gap[:], y2[:], MULT)
-        point_term = held.tile([P, N], F32, name="point_term")
-        nc.vector.tensor_tensor(point_term[:], gap[:], points[:], MULT)
+
+        coefficient_part = held.tile([P, N], F32, name="coefficient_part")
+        nc.vector.tensor_tensor(coefficient_part[:], coefficient[:], one_minus_y2[:], MULT)
+        distance_part = held.tile([P, N], F32, name="distance_part")
+        nc.vector.tensor_tensor(distance_part[:], distance_sum[:], y2[:], MULT)
         denominator = held.tile([P, N], F32, name="denominator")
-        nc.vector.tensor_tensor(denominator[:], coefficient[:], gap_y2[:], SUBTRACT)
-        numerator = held.tile([P, N], F32, name="numerator")
-        nc.vector.tensor_tensor(numerator[:], point_term[:], centre_term[:], SUBTRACT)
+        nc.vector.tensor_tensor(denominator[:], coefficient_part[:], distance_part[:], ADD)
         inverse = held.tile([P, N], F32, name="inverse")
         nc.vector.reciprocal(inverse[:], denominator[:])
+
+        gap = held.tile([P, N], F32, name="gap")
+        nc.vector.tensor_tensor(gap[:], coefficient[:], distance_sum[:], SUBTRACT)
+        point_term = held.tile([P, N], F32, name="point_term")
+        nc.vector.tensor_tensor(point_term[:], gap[:], points[:], MULT)
+        numerator = held.tile([P, N], F32, name="numerator")
+        nc.vector.tensor_tensor(numerator[:], point_term[:], centre_term[:], SUBTRACT)
 
         result = held.tile([P, N], F32, name="result")
         nc.vector.tensor_tensor(result[:], numerator[:], inverse[:], MULT)

@@ -37,6 +37,9 @@ def tile_factorizedjumpoperator_kernel(tc, centers, z, offs, out):
         minus_twos = held.tile([P, P], F32, name="minus_twos")
         nc.vector.memset(minus_twos[:], -2.0)
 
+        table_set_first = held.tile([P, 1], F32, name="table_set_first")
+        nc.scalar.activation(table_set_first[:], ones[:, 0:1], ACT.Abs_reciprocal_sqrt)
+
         minus_points = held.tile([P, N], F32, name="minus_points")
         nc.vector.tensor_scalar_mul(minus_points[:], points[:], -1.0)
         points_squared = held.tile([P, N], F32, name="points_squared")
@@ -73,8 +76,10 @@ def tile_factorizedjumpoperator_kernel(tc, centers, z, offs, out):
         nc.vector.tensor_tensor(distance_part[:], distance_sum[:], y2[:], MULT)
         denominator = held.tile([P, N], F32, name="denominator")
         nc.vector.tensor_tensor(denominator[:], coefficient_part[:], distance_part[:], ADD)
+        inverse_root = held.tile([P, N], F32, name="inverse_root")
+        nc.scalar.activation(inverse_root[:], denominator[:], ACT.Abs_reciprocal_sqrt)
         inverse = held.tile([P, N], F32, name="inverse")
-        nc.vector.reciprocal(inverse[:], denominator[:])
+        nc.scalar.activation(inverse[:], inverse_root[:], ACT.Square)
 
         gap = held.tile([P, N], F32, name="gap")
         nc.vector.tensor_tensor(gap[:], coefficient[:], distance_sum[:], SUBTRACT)

@@ -34,57 +34,59 @@ def tile_factorizedjumpoperator_kernel(tc, centers, z, offs, out):
 
         ones = held.tile([P, P], F32, name="ones")
         nc.vector.memset(ones[:], 1.0)
-        minus_twos = held.tile([P, P], F32, name="minus_twos")
-        nc.vector.memset(minus_twos[:], -2.0)
 
         table_set_first = held.tile([P, 1], F32, name="table_set_first")
         nc.scalar.activation(table_set_first[:], ones[:, 0:1], ACT.Abs_reciprocal_sqrt)
 
-        minus_points = held.tile([P, N], F32, name="minus_points")
-        nc.vector.tensor_scalar_mul(minus_points[:], points[:], -1.0)
+        minus_2_points = held.tile([P, N], F32, name="minus_2_points")
+        nc.vector.tensor_scalar_mul(minus_2_points[:], points[:], -2.0)
         points_squared = held.tile([P, N], F32, name="points_squared")
         nc.vector.tensor_tensor(points_squared[:], points[:], points[:], MULT)
         y2_sum = sums.tile([P, N], F32, name="y2_sum")
         nc.tensor.matmul(y2_sum[:], ones[:], points_squared[:], start=True, stop=True)
-        y2_plus_1 = held.tile([P, N], F32, name="y2_plus_1")
-        nc.scalar.activation(y2_plus_1[:], y2_sum[:], ACT.Copy, bias=1.0)
-        one_minus_y2 = held.tile([P, N], F32, name="one_minus_y2")
-        nc.scalar.activation(one_minus_y2[:], y2_sum[:], ACT.Copy, bias=1.0, scale=-1.0)
-        y2 = held.tile([P, N], F32, name="y2")
-        nc.scalar.activation(y2[:], y2_sum[:], ACT.Copy)
+
+        table_squared = held.tile([P, S], F32, name="table_squared")
+        for b in range(S // BLOCK):
+            block = slice(b * BLOCK, (b + 1) * BLOCK)
+            nc.scalar.activation(table_squared[:, block], table[:, block], ACT.Square)
 
         centre_times_point = held.tile([P, N], F32, name="centre_times_point")
-        nc.vector.tensor_tensor(centre_times_point[:], table[:].indirect(offsets[:]), points[:], MULT)
+        nc.vector.tensor_tensor(centre_times_point[:], table[:].indirect(offsets[:]), minus_2_points[:], MULT)
         minus_2cz_sum = sums.tile([P, N], F32, name="minus_2cz_sum")
-        nc.tensor.matmul(minus_2cz_sum[:], minus_twos[:], centre_times_point[:], start=True, stop=True)
+        nc.tensor.matmul(minus_2cz_sum[:], ones[:], centre_times_point[:], start=True, stop=True)
 
-        centre_minus_point = held.tile([P, N], F32, name="centre_minus_point")
-        nc.vector.tensor_tensor(centre_minus_point[:], table[:].indirect(offsets[:]), minus_points[:], ADD)
-        difference_squared = held.tile([P, N], F32, name="difference_squared")
-        nc.vector.tensor_tensor(difference_squared[:], centre_minus_point[:], centre_minus_point[:], MULT)
-        distance_sum = sums.tile([P, N], F32, name="distance_sum")
-        nc.tensor.matmul(distance_sum[:], ones[:], difference_squared[:], start=True, stop=True)
+        y2 = held.tile([P, N], F32, name="y2")
+        nc.vector.tensor_copy(y2[:], y2_sum[:])
+        y2_plus_1 = held.tile([P, N], F32, name="y2_plus_1")
+        nc.scalar.activation(y2_plus_1[:], y2_sum[:], ACT.Copy, bias=1.0)
+
+        square_times_y2 = held.tile([P, N], F32, name="square_times_y2")
+        nc.vector.tensor_tensor(square_times_y2[:], table_squared[:].indirect(offsets[:]), y2[:], MULT)
+        denominator_less_1 = sums.tile([P, N], F32, name="denominator_less_1")
+        nc.tensor.matmul(denominator_less_1[:], ones[:], centre_times_point[:], start=True, stop=False)
+        nc.tensor.matmul(denominator_less_1[:], ones[:], square_times_y2[:], start=False, stop=True)
 
         coefficient = held.tile([P, N], F32, name="coefficient")
         nc.vector.tensor_tensor(coefficient[:], y2_plus_1[:], minus_2cz_sum[:], ADD)
         centre_term = held.tile([P, N], F32, name="centre_term")
         nc.vector.tensor_tensor(centre_term[:], table[:].indirect(offsets[:]), coefficient[:], MULT)
 
-        coefficient_part = held.tile([P, N], F32, name="coefficient_part")
-        nc.vector.tensor_tensor(coefficient_part[:], coefficient[:], one_minus_y2[:], MULT)
-        distance_part = held.tile([P, N], F32, name="distance_part")
-        nc.vector.tensor_tensor(distance_part[:], distance_sum[:], y2[:], MULT)
-        denominator = held.tile([P, N], F32, name="denominator")
-        nc.vector.tensor_tensor(denominator[:], coefficient_part[:], distance_part[:], ADD)
+        y2_inverse_root = held.tile([P, N], F32, name="y2_inverse_root")
+        nc.scalar.activation(y2_inverse_root[:], y2_sum[:], ACT.Abs_reciprocal_sqrt)
+        y2_inverse = held.tile([P, N], F32, name="y2_inverse")
+        nc.scalar.activation(y2_inverse[:], y2_inverse_root[:], ACT.Square)
+        points_over_y2 = held.tile([P, N], F32, name="points_over_y2")
+        nc.vector.tensor_tensor(points_over_y2[:], points[:], y2_inverse[:], MULT)
+
         inverse_root = held.tile([P, N], F32, name="inverse_root")
-        nc.scalar.activation(inverse_root[:], denominator[:], ACT.Abs_reciprocal_sqrt)
+        nc.scalar.activation(inverse_root[:], denominator_less_1[:], ACT.Abs_reciprocal_sqrt, bias=1.0)
         inverse = held.tile([P, N], F32, name="inverse")
         nc.scalar.activation(inverse[:], inverse_root[:], ACT.Square)
 
-        gap = held.tile([P, N], F32, name="gap")
-        nc.vector.tensor_tensor(gap[:], coefficient[:], distance_sum[:], SUBTRACT)
+        gap_times_y2 = held.tile([P, N], F32, name="gap_times_y2")
+        nc.vector.scalar_tensor_tensor(gap_times_y2[:], coefficient[:], -1.0, denominator_less_1[:], ADD, SUBTRACT)
         point_term = held.tile([P, N], F32, name="point_term")
-        nc.vector.tensor_tensor(point_term[:], gap[:], points[:], MULT)
+        nc.vector.tensor_tensor(point_term[:], gap_times_y2[:], points_over_y2[:], MULT)
         numerator = held.tile([P, N], F32, name="numerator")
         nc.vector.tensor_tensor(numerator[:], point_term[:], centre_term[:], SUBTRACT)
 

@@ -15,16 +15,19 @@ FLOPS = 11 * P * N
 BYTES = 3 * P * N * 4 + P * (N // 16) * 2
 
 BLOCK = 256
+HALF = N // 2
 
 
 def tile_factorizedjumpoperator_kernel(tc, centers, z, offs, out):
     nc = tc.nc
+    halves = [slice(h * HALF, (h + 1) * HALF) for h in range(N // HALF)]
     with (
         tc.tile_pool(name="held", bufs=1) as held,
         tc.psum_pool(name="sums", bufs=1) as sums,
     ):
         offsets = held.tile([P, N // 16], U16, name="offsets")
         nc.sync.dma_start(offsets[:], offs)
+        lists = [offsets[:, h * (HALF // 16) : (h + 1) * (HALF // 16)] for h in range(N // HALF)]
         points = held.tile([P, N], F32, name="points")
         nc.scalar.dma_start(points[:], z)
         table = held.tile([P, S], F32, name="table")
@@ -41,55 +44,66 @@ def tile_factorizedjumpoperator_kernel(tc, centers, z, offs, out):
         minus_2_points = held.tile([P, N], F32, name="minus_2_points")
         nc.vector.tensor_scalar_mul(minus_2_points[:], points[:], -2.0)
         points_squared = held.tile([P, N], F32, name="points_squared")
-        nc.vector.tensor_tensor(points_squared[:], points[:], points[:], MULT)
-        y2_sum = sums.tile([P, N], F32, name="y2_sum")
-        nc.tensor.matmul(y2_sum[:], ones[:], points_squared[:], start=True, stop=True)
+        y2_sum = [sums.tile([P, HALF], F32, name=f"y2_sum{h}") for h in range(len(halves))]
+        for h, half in enumerate(halves):
+            nc.vector.tensor_tensor(points_squared[:, half], points[:, half], points[:, half], MULT)
+            nc.tensor.matmul(y2_sum[h][:], ones[:], points_squared[:, half], start=True, stop=True)
 
         table_squared = held.tile([P, S], F32, name="table_squared")
         for b in range(S // BLOCK):
             block = slice(b * BLOCK, (b + 1) * BLOCK)
             nc.scalar.activation(table_squared[:, block], table[:, block], ACT.Square)
 
-        centre_times_point = held.tile([P, N], F32, name="centre_times_point")
-        nc.vector.tensor_tensor(centre_times_point[:], table[:].indirect(offsets[:]), minus_2_points[:], MULT)
-        minus_2cz_sum = sums.tile([P, N], F32, name="minus_2cz_sum")
-        nc.tensor.matmul(minus_2cz_sum[:], ones[:], centre_times_point[:], start=True, stop=True)
-
         y2 = held.tile([P, N], F32, name="y2")
-        nc.vector.tensor_copy(y2[:], y2_sum[:])
-        y2_plus_1 = held.tile([P, N], F32, name="y2_plus_1")
-        nc.scalar.activation(y2_plus_1[:], y2_sum[:], ACT.Copy, bias=1.0)
+        for h, half in enumerate(halves):
+            nc.scalar.activation(y2[:, half], y2_sum[h][:], ACT.Copy)
+
+        centre_times_point = held.tile([P, N], F32, name="centre_times_point")
+        minus_2cz_sum = [sums.tile([P, HALF], F32, name=f"minus_2cz_sum{h}") for h in range(len(halves))]
+        for h, half in enumerate(halves):
+            nc.vector.tensor_tensor(centre_times_point[:, half], table[:].indirect(lists[h]), minus_2_points[:, half], MULT)
+            nc.tensor.matmul(minus_2cz_sum[h][:], ones[:], centre_times_point[:, half], start=True, stop=True)
 
         square_times_y2 = held.tile([P, N], F32, name="square_times_y2")
-        nc.vector.tensor_tensor(square_times_y2[:], table_squared[:].indirect(offsets[:]), y2[:], MULT)
-        denominator_less_1 = sums.tile([P, N], F32, name="denominator_less_1")
-        nc.tensor.matmul(denominator_less_1[:], ones[:], centre_times_point[:], start=True, stop=False)
-        nc.tensor.matmul(denominator_less_1[:], ones[:], square_times_y2[:], start=False, stop=True)
+        denominator_less_1 = [sums.tile([P, HALF], F32, name=f"denominator_less_1_{h}") for h in range(len(halves))]
+        for h, half in enumerate(halves):
+            nc.vector.tensor_tensor(square_times_y2[:, half], table_squared[:].indirect(lists[h]), y2[:, half], MULT)
+            nc.tensor.matmul(denominator_less_1[h][:], ones[:], centre_times_point[:, half], start=True, stop=False)
+            nc.tensor.matmul(denominator_less_1[h][:], ones[:], square_times_y2[:, half], start=False, stop=True)
 
         coefficient = held.tile([P, N], F32, name="coefficient")
-        nc.vector.tensor_tensor(coefficient[:], y2_plus_1[:], minus_2cz_sum[:], ADD)
+        for h, half in enumerate(halves):
+            nc.vector.scalar_tensor_tensor(coefficient[:, half], minus_2cz_sum[h][:], 1.0, y2[:, half], ADD, ADD)
         centre_term = held.tile([P, N], F32, name="centre_term")
-        nc.vector.tensor_tensor(centre_term[:], table[:].indirect(offsets[:]), coefficient[:], MULT)
+        for h, half in enumerate(halves):
+            nc.vector.tensor_tensor(centre_term[:, half], table[:].indirect(lists[h]), coefficient[:, half], MULT)
 
         y2_inverse_root = held.tile([P, N], F32, name="y2_inverse_root")
-        nc.scalar.activation(y2_inverse_root[:], y2_sum[:], ACT.Abs_reciprocal_sqrt)
+        nc.scalar.activation(y2_inverse_root[:], y2[:], ACT.Abs_reciprocal_sqrt)
         y2_inverse = held.tile([P, N], F32, name="y2_inverse")
         nc.scalar.activation(y2_inverse[:], y2_inverse_root[:], ACT.Square)
         points_over_y2 = held.tile([P, N], F32, name="points_over_y2")
         nc.vector.tensor_tensor(points_over_y2[:], points[:], y2_inverse[:], MULT)
 
         inverse_root = held.tile([P, N], F32, name="inverse_root")
-        nc.scalar.activation(inverse_root[:], denominator_less_1[:], ACT.Abs_reciprocal_sqrt, bias=1.0)
         inverse = held.tile([P, N], F32, name="inverse")
-        nc.scalar.activation(inverse[:], inverse_root[:], ACT.Square)
+        for h, half in enumerate(halves):
+            nc.scalar.activation(inverse_root[:, half], denominator_less_1[h][:], ACT.Abs_reciprocal_sqrt, bias=1.0)
+        for h, half in enumerate(halves):
+            nc.scalar.activation(inverse[:, half], inverse_root[:, half], ACT.Square)
 
         gap_times_y2 = held.tile([P, N], F32, name="gap_times_y2")
-        nc.vector.scalar_tensor_tensor(gap_times_y2[:], coefficient[:], -1.0, denominator_less_1[:], ADD, SUBTRACT)
+        for h, half in enumerate(halves):
+            nc.vector.scalar_tensor_tensor(gap_times_y2[:, half], coefficient[:, half], -1.0, denominator_less_1[h][:], ADD, SUBTRACT)
         point_term = held.tile([P, N], F32, name="point_term")
-        nc.vector.tensor_tensor(point_term[:], gap_times_y2[:], points_over_y2[:], MULT)
+        for h, half in enumerate(halves):
+            nc.vector.tensor_tensor(point_term[:, half], gap_times_y2[:, half], points_over_y2[:, half], MULT)
         numerator = held.tile([P, N], F32, name="numerator")
-        nc.vector.tensor_tensor(numerator[:], point_term[:], centre_term[:], SUBTRACT)
+        for h, half in enumerate(halves):
+            nc.vector.tensor_tensor(numerator[:, half], point_term[:, half], centre_term[:, half], SUBTRACT)
 
         result = held.tile([P, N], F32, name="result")
-        nc.vector.tensor_tensor(result[:], numerator[:], inverse[:], MULT)
-        nc.sync.dma_start(out, result[:])
+        for h, half in enumerate(halves):
+            nc.vector.tensor_tensor(result[:, half], numerator[:, half], inverse[:, half], MULT)
+            queue = nc.scalar if h == 0 else nc.sync
+            queue.dma_start(out[:, half], result[:, half])

@@ -41,13 +41,15 @@ def tile_factorizedjumpoperator_kernel(tc, centers, z, offs, out):
         table_set_first = held.tile([P, 1], F32, name="table_set_first")
         nc.scalar.activation(table_set_first[:], ones[:, 0:1], ACT.Abs_reciprocal_sqrt)
 
-        minus_2_points = held.tile([P, N], F32, name="minus_2_points")
-        nc.vector.tensor_scalar_mul(minus_2_points[:], points[:], -2.0)
         points_squared = held.tile([P, N], F32, name="points_squared")
         y2_sum = [sums.tile([P, HALF], F32, name=f"y2_sum{h}") for h in range(len(halves))]
         for h, half in enumerate(halves):
             nc.vector.tensor_tensor(points_squared[:, half], points[:, half], points[:, half], MULT)
             nc.tensor.matmul(y2_sum[h][:], ones[:], points_squared[:, half], start=True, stop=True)
+        minus_2_points = held.tile([P, N], F32, name="minus_2_points")
+        nc.vector.tensor_scalar_mul(minus_2_points[:], points[:], -2.0)
+        minus_points = held.tile([P, N], F32, name="minus_points")
+        nc.vector.tensor_scalar_mul(minus_points[:], points[:], -1.0)
 
         table_squared = held.tile([P, S], F32, name="table_squared")
         for b in range(S // BLOCK):
@@ -65,39 +67,39 @@ def tile_factorizedjumpoperator_kernel(tc, centers, z, offs, out):
             nc.tensor.matmul(minus_2cz_sum[h][:], ones[:], centre_times_point[:, half], start=True, stop=True)
 
         square_times_y2 = held.tile([P, N], F32, name="square_times_y2")
-        denominator_less_1 = [sums.tile([P, HALF], F32, name=f"denominator_less_1_{h}") for h in range(len(halves))]
+        x2_y2_sum = [sums.tile([P, HALF], F32, name=f"x2_y2_sum{h}") for h in range(len(halves))]
         for h, half in enumerate(halves):
             nc.vector.tensor_tensor(square_times_y2[:, half], table_squared[:].indirect(lists[h]), y2[:, half], MULT)
-            nc.tensor.matmul(denominator_less_1[h][:], ones[:], centre_times_point[:, half], start=True, stop=False)
-            nc.tensor.matmul(denominator_less_1[h][:], ones[:], square_times_y2[:, half], start=False, stop=True)
-
-        coefficient = held.tile([P, N], F32, name="coefficient")
-        for h, half in enumerate(halves):
-            nc.vector.scalar_tensor_tensor(coefficient[:, half], minus_2cz_sum[h][:], 1.0, y2[:, half], ADD, ADD)
-        centre_term = held.tile([P, N], F32, name="centre_term")
-        for h, half in enumerate(halves):
-            nc.vector.tensor_tensor(centre_term[:, half], table[:].indirect(lists[h]), coefficient[:, half], MULT)
+            nc.tensor.matmul(x2_y2_sum[h][:], ones[:], square_times_y2[:, half], start=True, stop=True)
 
         y2_inverse_root = held.tile([P, N], F32, name="y2_inverse_root")
         nc.scalar.activation(y2_inverse_root[:], y2[:], ACT.Abs_reciprocal_sqrt)
         y2_inverse = held.tile([P, N], F32, name="y2_inverse")
         nc.scalar.activation(y2_inverse[:], y2_inverse_root[:], ACT.Square)
-        points_over_y2 = held.tile([P, N], F32, name="points_over_y2")
-        nc.vector.tensor_tensor(points_over_y2[:], points[:], y2_inverse[:], MULT)
 
+        coefficient = held.tile([P, N], F32, name="coefficient")
+        one_minus_2cz = held.tile([P, N], F32, name="one_minus_2cz")
+        for h, half in enumerate(halves):
+            nc.vector.scalar_tensor_tensor(coefficient[:, half], minus_2cz_sum[h][:], 1.0, y2[:, half], ADD, ADD)
+            nc.scalar.activation(one_minus_2cz[:, half], minus_2cz_sum[h][:], ACT.Copy, bias=1.0)
+        centre_term = held.tile([P, N], F32, name="centre_term")
+        for h, half in enumerate(halves):
+            nc.vector.tensor_tensor(centre_term[:, half], table[:].indirect(lists[h]), coefficient[:, half], MULT)
+
+        x2 = held.tile([P, N], F32, name="x2")
+        denominator = held.tile([P, N], F32, name="denominator")
         inverse_root = held.tile([P, N], F32, name="inverse_root")
         inverse = held.tile([P, N], F32, name="inverse")
         for h, half in enumerate(halves):
-            nc.scalar.activation(inverse_root[:, half], denominator_less_1[h][:], ACT.Abs_reciprocal_sqrt, bias=1.0)
+            nc.vector.tensor_tensor(x2[:, half], x2_y2_sum[h][:], y2_inverse[:, half], MULT)
+            nc.vector.tensor_tensor(denominator[:, half], x2_y2_sum[h][:], one_minus_2cz[:, half], ADD)
+            nc.scalar.activation(inverse_root[:, half], denominator[:, half], ACT.Abs_reciprocal_sqrt)
         for h, half in enumerate(halves):
             nc.scalar.activation(inverse[:, half], inverse_root[:, half], ACT.Square)
 
-        gap_times_y2 = held.tile([P, N], F32, name="gap_times_y2")
-        for h, half in enumerate(halves):
-            nc.vector.scalar_tensor_tensor(gap_times_y2[:, half], coefficient[:, half], -1.0, denominator_less_1[h][:], ADD, SUBTRACT)
         point_term = held.tile([P, N], F32, name="point_term")
         for h, half in enumerate(halves):
-            nc.vector.tensor_tensor(point_term[:, half], gap_times_y2[:, half], points_over_y2[:, half], MULT)
+            nc.vector.scalar_tensor_tensor(point_term[:, half], x2[:, half], -1.0, minus_points[:, half], ADD, MULT)
         numerator = held.tile([P, N], F32, name="numerator")
         for h, half in enumerate(halves):
             nc.vector.tensor_tensor(numerator[:, half], point_term[:, half], centre_term[:, half], SUBTRACT)

@@ -37,6 +37,8 @@ def tile_factorizedjumpoperator_kernel(tc, centers, z, offs, out):
 
         ones = held.tile([P, P], F32, name="ones")
         nc.vector.memset(ones[:], 1.0)
+        minus_ones = held.tile([P, P], F32, name="minus_ones")
+        nc.vector.memset(minus_ones[:], -1.0)
 
         table_set_first = held.tile([P, 1], F32, name="table_set_first")
         nc.scalar.activation(table_set_first[:], ones[:, 0:1], ACT.Abs_reciprocal_sqrt)
@@ -48,8 +50,6 @@ def tile_factorizedjumpoperator_kernel(tc, centers, z, offs, out):
             nc.tensor.matmul(y2_sum[h][:], ones[:], points_squared[:, half], start=True, stop=True)
         minus_2_points = held.tile([P, N], F32, name="minus_2_points")
         nc.vector.tensor_scalar_mul(minus_2_points[:], points[:], -2.0)
-        minus_points = held.tile([P, N], F32, name="minus_points")
-        nc.vector.tensor_scalar_mul(minus_points[:], points[:], -1.0)
 
         table_squared = held.tile([P, S], F32, name="table_squared")
         for b in range(S // BLOCK):
@@ -57,8 +57,15 @@ def tile_factorizedjumpoperator_kernel(tc, centers, z, offs, out):
             nc.scalar.activation(table_squared[:, block], table[:, block], ACT.Square)
 
         y2 = held.tile([P, N], F32, name="y2")
+        y2_inverse_root = held.tile([P, N], F32, name="y2_inverse_root")
+        y2_inverse = [held.tile([P, HALF], F32, name=f"y2_inverse{h}", tag=f"inverse_then_coefficient{h}") for h in range(len(halves))]
         for h, half in enumerate(halves):
+            nc.scalar.activation(y2_inverse_root[:, half], y2_sum[h][:], ACT.Abs_reciprocal_sqrt)
             nc.scalar.activation(y2[:, half], y2_sum[h][:], ACT.Copy)
+            nc.scalar.activation(y2_inverse[h][:], y2_inverse_root[:, half], ACT.Square)
+        points_over_y2 = held.tile([P, N], F32, name="points_over_y2")
+        for h, half in enumerate(halves):
+            nc.vector.tensor_tensor(points_over_y2[:, half], points[:, half], y2_inverse[h][:], MULT)
 
         centre_times_point = held.tile([P, N], F32, name="centre_times_point")
         minus_2cz_sum = [sums.tile([P, HALF], F32, name=f"minus_2cz_sum{h}") for h in range(len(halves))]
@@ -67,39 +74,31 @@ def tile_factorizedjumpoperator_kernel(tc, centers, z, offs, out):
             nc.tensor.matmul(minus_2cz_sum[h][:], ones[:], centre_times_point[:, half], start=True, stop=True)
 
         square_times_y2 = held.tile([P, N], F32, name="square_times_y2")
-        x2_y2_sum = [sums.tile([P, HALF], F32, name=f"x2_y2_sum{h}") for h in range(len(halves))]
+        gap = [sums.tile([P, HALF], F32, name=f"gap{h}") for h in range(len(halves))]
+        for h, half in enumerate(halves):
+            nc.tensor.matmul(gap[h][:], ones[:], points_squared[:, half], start=True, stop=False)
         for h, half in enumerate(halves):
             nc.vector.tensor_tensor(square_times_y2[:, half], table_squared[:].indirect(lists[h]), y2[:, half], MULT)
-            nc.tensor.matmul(x2_y2_sum[h][:], ones[:], square_times_y2[:, half], start=True, stop=True)
+            nc.tensor.matmul(gap[h][:], minus_ones[:], square_times_y2[:, half], start=False, stop=True)
 
-        y2_inverse_root = held.tile([P, N], F32, name="y2_inverse_root")
-        nc.scalar.activation(y2_inverse_root[:], y2[:], ACT.Abs_reciprocal_sqrt)
-        y2_inverse = held.tile([P, N], F32, name="y2_inverse")
-        nc.scalar.activation(y2_inverse[:], y2_inverse_root[:], ACT.Square)
-
-        coefficient = held.tile([P, N], F32, name="coefficient")
-        one_minus_2cz = held.tile([P, N], F32, name="one_minus_2cz")
+        coefficient = [held.tile([P, HALF], F32, name=f"coefficient{h}", tag=f"inverse_then_coefficient{h}") for h in range(len(halves))]
         for h, half in enumerate(halves):
-            nc.vector.scalar_tensor_tensor(coefficient[:, half], minus_2cz_sum[h][:], 1.0, y2[:, half], ADD, ADD)
-            nc.scalar.activation(one_minus_2cz[:, half], minus_2cz_sum[h][:], ACT.Copy, bias=1.0)
+            nc.vector.scalar_tensor_tensor(coefficient[h][:], minus_2cz_sum[h][:], 1.0, y2[:, half], ADD, ADD)
         centre_term = held.tile([P, N], F32, name="centre_term")
         for h, half in enumerate(halves):
-            nc.vector.tensor_tensor(centre_term[:, half], table[:].indirect(lists[h]), coefficient[:, half], MULT)
+            nc.vector.tensor_tensor(centre_term[:, half], table[:].indirect(lists[h]), coefficient[h][:], MULT)
 
-        x2 = held.tile([P, N], F32, name="x2")
         denominator = held.tile([P, N], F32, name="denominator")
+        point_term = held.tile([P, N], F32, name="point_term")
         inverse_root = held.tile([P, N], F32, name="inverse_root")
         inverse = held.tile([P, N], F32, name="inverse")
         for h, half in enumerate(halves):
-            nc.vector.tensor_tensor(x2[:, half], x2_y2_sum[h][:], y2_inverse[:, half], MULT)
-            nc.vector.tensor_tensor(denominator[:, half], x2_y2_sum[h][:], one_minus_2cz[:, half], ADD)
+            nc.vector.tensor_tensor(denominator[:, half], coefficient[h][:], gap[h][:], SUBTRACT)
             nc.scalar.activation(inverse_root[:, half], denominator[:, half], ACT.Abs_reciprocal_sqrt)
+            nc.vector.tensor_tensor(point_term[:, half], gap[h][:], points_over_y2[:, half], MULT)
         for h, half in enumerate(halves):
             nc.scalar.activation(inverse[:, half], inverse_root[:, half], ACT.Square)
 
-        point_term = held.tile([P, N], F32, name="point_term")
-        for h, half in enumerate(halves):
-            nc.vector.scalar_tensor_tensor(point_term[:, half], x2[:, half], -1.0, minus_points[:, half], ADD, MULT)
         numerator = held.tile([P, N], F32, name="numerator")
         for h, half in enumerate(halves):
             nc.vector.tensor_tensor(numerator[:, half], point_term[:, half], centre_term[:, half], SUBTRACT)

@@ -44,7 +44,7 @@ def tile_factorizedjumpoperator_kernel(tc, centers, z, offs, out):
         nc.scalar.activation(table_set_first[:], ones[:, 0:1], ACT.Abs_reciprocal_sqrt)
 
         points_squared = held.tile([P, N], F32, name="points_squared")
-        y2_sum = [sums.tile([P, HALF], F32, name=f"y2_sum{h}") for h in range(len(halves))]
+        y2_sum = [sums.tile([P, HALF], F32, name=f"y2_sum{h}", tag=f"y2_then_gap{h}") for h in range(len(halves))]
         for h, half in enumerate(halves):
             nc.vector.tensor_tensor(points_squared[:, half], points[:, half], points[:, half], MULT)
             nc.tensor.matmul(y2_sum[h][:], ones[:], points_squared[:, half], start=True, stop=True)
@@ -74,7 +74,7 @@ def tile_factorizedjumpoperator_kernel(tc, centers, z, offs, out):
             nc.tensor.matmul(minus_2cz_sum[h][:], ones[:], centre_times_point[:, half], start=True, stop=True)
 
         square_times_y2 = held.tile([P, N], F32, name="square_times_y2")
-        gap = [sums.tile([P, HALF], F32, name=f"gap{h}") for h in range(len(halves))]
+        gap = [sums.tile([P, HALF], F32, name=f"gap{h}", tag=f"y2_then_gap{h}") for h in range(len(halves))]
         for h, half in enumerate(halves):
             nc.tensor.matmul(gap[h][:], ones[:], points_squared[:, half], start=True, stop=False)
         for h, half in enumerate(halves):

@@ -58,14 +58,14 @@ def tile_factorizedjumpoperator_kernel(tc, centers, z, offs, out):
 
         y2 = held.tile([P, N], F32, name="y2")
         y2_inverse_root = held.tile([P, N], F32, name="y2_inverse_root")
-        y2_inverse = [held.tile([P, HALF], F32, name=f"y2_inverse{h}", tag=f"inverse_then_coefficient{h}") for h in range(len(halves))]
+        y2_inverse = held.tile([P, N], F32, name="y2_inverse")
         for h, half in enumerate(halves):
             nc.scalar.activation(y2_inverse_root[:, half], y2_sum[h][:], ACT.Abs_reciprocal_sqrt)
             nc.scalar.activation(y2[:, half], y2_sum[h][:], ACT.Copy)
-            nc.scalar.activation(y2_inverse[h][:], y2_inverse_root[:, half], ACT.Square)
+            nc.scalar.activation(y2_inverse[:, half], y2_inverse_root[:, half], ACT.Square)
         points_over_y2 = held.tile([P, N], F32, name="points_over_y2")
         for h, half in enumerate(halves):
-            nc.vector.tensor_tensor(points_over_y2[:, half], points[:, half], y2_inverse[h][:], MULT)
+            nc.gpsimd.tensor_tensor(points_over_y2[:, half], points[:, half], y2_inverse[:, half], MULT)
 
         centre_times_point = held.tile([P, N], F32, name="centre_times_point")
         minus_2cz_sum = [sums.tile([P, HALF], F32, name=f"minus_2cz_sum{h}") for h in range(len(halves))]
@@ -81,19 +81,19 @@ def tile_factorizedjumpoperator_kernel(tc, centers, z, offs, out):
             nc.vector.tensor_tensor(square_times_y2[:, half], table_squared[:].indirect(lists[h]), y2[:, half], MULT)
             nc.tensor.matmul(gap[h][:], minus_ones[:], square_times_y2[:, half], start=False, stop=True)
 
-        coefficient = [held.tile([P, HALF], F32, name=f"coefficient{h}", tag=f"inverse_then_coefficient{h}") for h in range(len(halves))]
+        coefficient = held.tile([P, N], F32, name="coefficient")
         for h, half in enumerate(halves):
-            nc.vector.scalar_tensor_tensor(coefficient[h][:], minus_2cz_sum[h][:], 1.0, y2[:, half], ADD, ADD)
+            nc.vector.scalar_tensor_tensor(coefficient[:, half], minus_2cz_sum[h][:], 1.0, y2[:, half], ADD, ADD)
         centre_term = held.tile([P, N], F32, name="centre_term")
         for h, half in enumerate(halves):
-            nc.vector.tensor_tensor(centre_term[:, half], table[:].indirect(lists[h]), coefficient[h][:], MULT)
+            nc.vector.tensor_tensor(centre_term[:, half], table[:].indirect(lists[h]), coefficient[:, half], MULT)
 
         denominator = held.tile([P, N], F32, name="denominator")
         point_term = held.tile([P, N], F32, name="point_term")
         inverse_root = held.tile([P, N], F32, name="inverse_root")
         inverse = held.tile([P, N], F32, name="inverse")
         for h, half in enumerate(halves):
-            nc.vector.tensor_tensor(denominator[:, half], coefficient[h][:], gap[h][:], SUBTRACT)
+            nc.vector.tensor_tensor(denominator[:, half], coefficient[:, half], gap[h][:], SUBTRACT)
             nc.scalar.activation(inverse_root[:, half], denominator[:, half], ACT.Abs_reciprocal_sqrt)
             nc.vector.tensor_tensor(point_term[:, half], gap[h][:], points_over_y2[:, half], MULT)
         for h, half in enumerate(halves):

import concourse.mybir as mybir

P = 128
S = 1024
N = 256

F32 = mybir.dt.float32
U16 = mybir.dt.uint16
MULT = mybir.AluOpType.mult
ADD = mybir.AluOpType.add
SUBTRACT = mybir.AluOpType.subtract
ACT = mybir.ActivationFunctionType

FLOPS = 11 * P * N
BYTES = 3 * P * N * 4 + P * (N // 16) * 2

BLOCK = 256
HALF = N // 2


def tile_factorizedjumpoperator_kernel(tc, centers, z, offs, out):
    nc = tc.nc
    halves = [slice(h * HALF, (h + 1) * HALF) for h in range(N // HALF)]
    with (
        tc.tile_pool(name="held", bufs=1) as held,
        tc.psum_pool(name="sums", bufs=1) as sums,
    ):
        offsets = held.tile([P, N // 16], U16, name="offsets")
        nc.sync.dma_start(offsets[:], offs)
        lists = [offsets[:, h * (HALF // 16) : (h + 1) * (HALF // 16)] for h in range(N // HALF)]
        points = held.tile([P, N], F32, name="points")
        nc.scalar.dma_start(points[:], z)
        table = held.tile([P, S], F32, name="table")
        for b in range(S // BLOCK):
            queue = nc.sync if b % 2 == 0 else nc.scalar
            queue.dma_start(table[:, b * BLOCK : (b + 1) * BLOCK], centers[:, b * BLOCK : (b + 1) * BLOCK])

        ones = held.tile([P, P], F32, name="ones")
        nc.vector.memset(ones[:], 1.0)
        minus_ones = held.tile([P, P], F32, name="minus_ones")
        nc.vector.memset(minus_ones[:], -1.0)

        table_set_first = held.tile([P, 1], F32, name="table_set_first")
        nc.scalar.activation(table_set_first[:], ones[:, 0:1], ACT.Abs_reciprocal_sqrt)

        points_squared = held.tile([P, N], F32, name="points_squared")
        y2_sum = [sums.tile([P, HALF], F32, name=f"y2_sum{h}", tag=f"y2_then_gap{h}") for h in range(len(halves))]
        for h, half in enumerate(halves):
            nc.vector.tensor_tensor(points_squared[:, half], points[:, half], points[:, half], MULT)
            nc.tensor.matmul(y2_sum[h][:], ones[:], points_squared[:, half], start=True, stop=True)
        minus_2_points = held.tile([P, N], F32, name="minus_2_points")
        nc.vector.tensor_scalar_mul(minus_2_points[:], points[:], -2.0)

        table_squared = held.tile([P, S], F32, name="table_squared")
        for b in range(S // BLOCK):
            block = slice(b * BLOCK, (b + 1) * BLOCK)
            nc.scalar.activation(table_squared[:, block], table[:, block], ACT.Square)

        y2 = held.tile([P, N], F32, name="y2")
        y2_inverse_root = held.tile([P, N], F32, name="y2_inverse_root")
        y2_inverse = held.tile([P, N], F32, name="y2_inverse")
        for h, half in enumerate(halves):
            nc.scalar.activation(y2_inverse_root[:, half], y2_sum[h][:], ACT.Abs_reciprocal_sqrt)
            nc.scalar.activation(y2[:, half], y2_sum[h][:], ACT.Copy)
            nc.scalar.activation(y2_inverse[:, half], y2_inverse_root[:, half], ACT.Square)
        points_over_y2 = held.tile([P, N], F32, name="points_over_y2")
        for h, half in enumerate(halves):
            nc.gpsimd.tensor_tensor(points_over_y2[:, half], points[:, half], y2_inverse[:, half], MULT)

        centre_times_point = held.tile([P, N], F32, name="centre_times_point")
        minus_2cz_sum = [sums.tile([P, HALF], F32, name=f"minus_2cz_sum{h}") for h in range(len(halves))]
        for h, half in enumerate(halves):
            nc.vector.tensor_tensor(centre_times_point[:, half], table[:].indirect(lists[h]), minus_2_points[:, half], MULT)
            nc.tensor.matmul(minus_2cz_sum[h][:], ones[:], centre_times_point[:, half], start=True, stop=True)

        square_times_y2 = held.tile([P, N], F32, name="square_times_y2")
        gap = [sums.tile([P, HALF], F32, name=f"gap{h}", tag=f"y2_then_gap{h}") for h in range(len(halves))]
        for h, half in enumerate(halves):
            nc.tensor.matmul(gap[h][:], ones[:], points_squared[:, half], start=True, stop=False)
        for h, half in enumerate(halves):
            nc.vector.tensor_tensor(square_times_y2[:, half], table_squared[:].indirect(lists[h]), y2[:, half], MULT)
            nc.tensor.matmul(gap[h][:], minus_ones[:], square_times_y2[:, half], start=False, stop=True)

        coefficient = held.tile([P, N], F32, name="coefficient")
        for h, half in enumerate(halves):
            nc.vector.scalar_tensor_tensor(coefficient[:, half], minus_2cz_sum[h][:], 1.0, y2[:, half], ADD, ADD)
        centre_term = held.tile([P, N], F32, name="centre_term")
        for h, half in enumerate(halves):
            nc.vector.tensor_tensor(centre_term[:, half], table[:].indirect(lists[h]), coefficient[:, half], MULT)

        denominator = held.tile([P, N], F32, name="denominator")
        point_term = held.tile([P, N], F32, name="point_term")
        inverse_root = held.tile([P, N], F32, name="inverse_root")
        inverse = held.tile([P, N], F32, name="inverse")
        for h, half in enumerate(halves):
            nc.vector.tensor_tensor(denominator[:, half], coefficient[:, half], gap[h][:], SUBTRACT)
            nc.scalar.activation(inverse_root[:, half], denominator[:, half], ACT.Abs_reciprocal_sqrt)
            nc.vector.tensor_tensor(point_term[:, half], gap[h][:], points_over_y2[:, half], MULT)
        for h, half in enumerate(halves):
            nc.scalar.activation(inverse[:, half], inverse_root[:, half], ACT.Square)

        numerator = held.tile([P, N], F32, name="numerator")
        for h, half in enumerate(halves):
            nc.vector.tensor_tensor(numerator[:, half], point_term[:, half], centre_term[:, half], SUBTRACT)

        result = held.tile([P, N], F32, name="result")
        for h, half in enumerate(halves):
            nc.vector.tensor_tensor(result[:, half], numerator[:, half], inverse[:, half], MULT)
            queue = nc.scalar if h == 0 else nc.sync
            queue.dma_start(out[:, half], result[:, half])
